import numpy as np
import ml_dtypes


def mxq(x, axis, fmt="e4m3"):
    dtype, down = {"e4m3": (ml_dtypes.float8_e4m3fn, 7), "e5m2": (ml_dtypes.float8_e5m2, 14)}[fmt]
    v = np.moveaxis(np.asarray(x, np.float32).astype(ml_dtypes.bfloat16).astype(np.float64), axis, -1)
    blocks = v.reshape(v.shape[:-1] + (-1, 32))
    amax = np.abs(blocks).max(-1, keepdims=True)
    byte = np.maximum(np.where(amax > 0, np.frexp(amax)[1] - 1 + 127, 0) - down, 1)
    scale = np.exp2(byte - 127.0)
    codes = (blocks / scale).astype(np.float32).astype(dtype).astype(np.float64)
    return np.moveaxis((codes * scale).reshape(v.shape), -1, axis)


WIDE = False


def mx_kscale(k):
    if not WIDE:
        return np.ones(k)
    levels = np.array([18, -18])
    if k % 512:
        return np.exp2(np.random.permutation(np.resize(levels, k // 32))).repeat(32)
    a = np.empty((k // 512, 16))
    for p in range(k // 512):
        a[p, :8] = np.random.permutation(np.resize(levels, 8))
        for g in range(8):
            far = levels[np.abs(levels - a[p, g]) >= 10]
            a[p, g + 8] = far[np.random.randint(len(far))]
    return np.exp2(a.ravel()).repeat(32)


BF16 = ml_dtypes.bfloat16


def bf(x):
    return np.asarray(x, np.float32).astype(BF16)


def f64(x):
    return np.asarray(x).astype(np.float64)


B, L, IN_F, OUT_F = 4, 2048, 512, 512
SCALE = 1.0 / np.sqrt(IN_F)
EPS = 1e-8


def demod(y, weight):
    w = SCALE * f64(weight) * f64(y)[:, None, :]
    return 1.0 / np.sqrt(np.sum(w * w, axis=2) + EPS)


def setup_inputs():
    s = mx_kscale(L)
    u = mx_kscale(OUT_F)
    xr0 = bf(np.random.standard_normal((B, IN_F, L)))
    y = bf(np.random.standard_normal((B, IN_F)))
    w0 = bf(np.random.standard_normal((1, OUT_F, IN_F)))
    dconf = demod(y, w0)
    g = np.random.standard_normal((B, OUT_F, L)) * np.exp2(np.random.randint(-6, 1, (B, 1, L)))
    g = bf(g * u[None, :, None] / s[None, None, :])
    return {"Efou": bf(f64(xr0) * s[None, None, :]).reshape(B, L, IN_F), "y": y,
            "weight": bf(f64(w0) / u[None, :, None]),
            "dconf": np.asarray(dconf, np.float32), "grad_out": g.reshape(B, L, OUT_F)}


def reference(Efou, y, weight, dconf, grad_out):
    Efou, y, weight, dc, g = f64(Efou), f64(y), f64(weight), f64(dconf), f64(grad_out)
    b, size_patch, in_f = Efou.shape
    out_f = weight.shape[1]
    Xr = Efou.reshape(b, in_f, size_patch)
    G = g.reshape(b, out_f, size_patch)
    wd = SCALE * weight * y[:, None, :] * dc[:, :, None]
    dXr = mxq(wd, 1, "e4m3").transpose(0, 2, 1) @ mxq(G, 1, "e5m2")
    dwd = mxq(G, 2, "e5m2") @ mxq(Xr, 2, "e4m3").transpose(0, 2, 1)
    t = np.sum(dwd * wd, axis=2)
    dw = dc[:, :, None] * (dwd - wd * t[:, :, None])
    dweight = SCALE * np.sum(dw * y[:, None, :], axis=0)[None]
    return dXr.reshape(b, size_patch, in_f), dweight

@@ -1,0 +1,333 @@
+import math
+from contextlib import ExitStack
+
+import concourse.mybir as mybir
+from concourse.masks import make_identity
+
+B, L, IN_F, OUT_F = 4, 2048, 512, 512
+SCALE = 1.0 / math.sqrt(IN_F)
+FLOPS = 2 * 2 * B * OUT_F * IN_F * L
+
+F32 = mybir.dt.float32
+BF16 = mybir.dt.bfloat16
+U32 = mybir.dt.uint32
+U8 = mybir.dt.uint8
+E4 = mybir.dt.float8_e4m3fn_x4
+E5 = mybir.dt.float8_e5m2_x4
+MULT = mybir.AluOpType.mult
+ADD = mybir.AluOpType.add
+SUB = mybir.AluOpType.subtract
+
+P = 128
+PACK = 4
+CHUNK = 512
+CHUNKS_PER_B = L // CHUNK
+N_CHUNKS = B * CHUNKS_PER_B
+N_HALVES = 2 * N_CHUNKS
+RAW_BUFS = 4
+DX_LAG = 7
+DW_LAG = 9
+EPI_LAG = 5
+
+
+def tile_modulatedlinear2_v_kernel(tc, Efou, y, weight, dconf, grad_out, out_0, out_1):
+    nc = tc.nc
+    g_hbm = grad_out.rearrange("b (q j a) f -> b q j (a f)", j=PACK, a=CHUNKS_PER_B)
+    x_hbm = Efou.rearrange("b (c r a) f -> b r c (a f)", r=P, a=CHUNKS_PER_B)
+    dx_hbm = out_0.rearrange("b (i a) f -> b i (a f)", a=CHUNKS_PER_B)
+    w_hbm = weight.rearrange("z (q j) i -> (z q) j i", j=PACK)
+    dweight_hbm = out_1.rearrange("z (q j) i -> (z q) j i", j=PACK)
+
+    units = [(0, 1), (1, 1)] + [(s, 2) for s in range(2, N_CHUNKS, 2)]
+    unit_of_chunk = {s: n for n, (first, count) in enumerate(units) for s in range(first, first + count)}
+
+    with ExitStack() as ctx:
+        keep = ctx.enter_context(tc.tile_pool(name="keep", bufs=1))
+        work = ctx.enter_context(tc.tile_pool(name="work", bufs=2))
+        psum = ctx.enter_context(tc.psum_pool(name="psum", bufs=2))
+        ctx.enter_context(tc.manual_schedule())
+
+        raw = {"g": {}, "x": {}}
+        staged = {}
+        g_by_o = {}
+        by_p = {"g": {}, "x": {}}
+        wd_rows, wd_staged, wd_q = {}, {}, {}
+        dwd_bank, u_tile, a_rows, r_bank, corr = {}, {}, {}, {}, {}
+
+        def load_unit(kind, n):
+            first, count = units[n]
+            b, g = divmod(first, CHUNKS_PER_B)
+            hbm = g_hbm if kind == "g" else x_hbm
+            t = work.tile([P, PACK, count * CHUNK], BF16, name="raw_" + kind, tag="raw_" + kind, bufs=RAW_BUFS)
+            nc.sync.dma_start(out=t[:], in_=hbm[b, :, :, g * CHUNK : (g + count) * CHUNK])
+            raw[kind][n] = t
+
+        def raw_offset(s):
+            n = unit_of_chunk[s]
+            return n, (s - units[n][0]) * CHUNK
+
+        def quantise(src, fmt, tag, bufs):
+            codes = work.tile([P, CHUNK], U32, name=tag + "_codes", tag=tag + "_codes", bufs=bufs, align_bytes=64)
+            scales = work.tile([P, CHUNK], U8, name=tag + "_scales", tag=tag + "_scales", bufs=bufs, align_bytes=64)
+            nc.vector.quantize_mx(out=codes[:].bitcast(fmt), scales=scales[:], in_=src[:])
+            return codes, scales, fmt
+
+        def mx_pass(out, stationary, block, moving, start, stop):
+            cols = slice(block * P, (block + 1) * P)
+            nc.tensor.matmul_mx(
+                out=out,
+                lhsT=stationary[0][:, cols].bitcast(stationary[2]),
+                lhsT_scale=stationary[1][:, cols],
+                rhs=moving[0][:].bitcast(moving[2]),
+                rhs_scale=moving[1][:],
+                start=start,
+                stop=stop,
+            )
+
+        def interleave_views(dst, src):
+            return (
+                dst.rearrange("p (c i t) -> p c t i", i=4, t=PACK),
+                src.rearrange("p t (c i) -> p c t i", i=4),
+            )
+
+        def interleave_g(s):
+            n, off = raw_offset(s)
+            t = work.tile([P, PACK * CHUNK], BF16, name="g_grouped", tag="g_grouped", bufs=2, align_bytes=64)
+            dst, src = interleave_views(t[:], raw["g"][n][:, :, off : off + CHUNK])
+            nc.vector.tensor_copy(out=dst, in_=src)
+            staged["i", s] = t
+
+        def quantise_g_by_o(s):
+            g_by_o[s] = quantise(staged["i", s], E5, "g_by_o", 8)
+
+        def transpose_chunk(kind, s):
+            n, off = raw_offset(s)
+            t = work.tile([P, PACK * CHUNK], BF16, name="turned_" + kind, tag="turned_" + kind, bufs=3, align_bytes=64)
+            t_words = t[:].bitcast(F32).rearrange("p (j q u) -> p j q u", j=PACK, u=2)
+            banks = []
+            for pair in range(2):
+                bank = psum.tile([P, 2, 2, P], F32, name="turn_bank", tag="turn_bank", bufs=4)
+                for jj in range(2):
+                    words = raw[kind][n][:, 2 * pair + jj, off : off + CHUNK].bitcast(F32)
+                    for u in range(2):
+                        nc.tensor.transpose(bank[:, jj, u, :], words[:, u : CHUNK // 2 : 2], ident_f32[:])
+                banks.append(bank)
+            for pair in range(2):
+                nc.scalar.copy(
+                    out=t_words[:, 2 * pair : 2 * pair + 2, :, :],
+                    in_=banks[pair][:].rearrange("p j u q -> p j q u"),
+                )
+            staged[kind, s] = t
+
+        def quantise_by_p(kind, s):
+            by_p[kind][s] = quantise(staged[kind, s], E5 if kind == "g" else E4, kind + "_by_p", 8)
+
+        def wd_piece(b, j):
+            if j == 0:
+                wd_rows[b] = work.tile([P, PACK, IN_F], BF16, name="wd_rows", tag="wd_rows", bufs=2)
+            nc.vector.scalar_tensor_tensor(
+                out=wd_rows[b][:, j, :], in0=w_sb[:, j, :], scalar=dc_scaled[:, b, j : j + 1],
+                in1=y_wide[:, b, :], op0=MULT, op1=MULT,
+            )
+
+        def wd_interleave(b, quarter):
+            if quarter == 0:
+                wd_staged[b] = work.tile([P, PACK * IN_F], BF16, name="wd_grouped", tag="wd_grouped", bufs=2, align_bytes=64)
+            dst, src = interleave_views(
+                wd_staged[b][:, quarter * PACK * P : (quarter + 1) * PACK * P],
+                wd_rows[b][:, :, quarter * P : (quarter + 1) * P],
+            )
+            nc.scalar.copy(out=dst, in_=src)
+
+        def dx_pair(m):
+            b, rest = divmod(m, 8)
+            half, c = divmod(rest, 4)
+            first = b * CHUNKS_PER_B + 2 * half
+            banks = []
+            for e in range(2):
+                bank = psum.tile([P, CHUNK], F32, name="dx_bank", tag="dx_bank", bufs=2)
+                mx_pass(bank[:], wd_q[b], c, g_by_o[first + e], True, True)
+                banks.append(bank)
+            result = work.tile([P, 2 * CHUNK], F32, name="dx_out", tag="dx_out", bufs=4)
+            for e in range(2):
+                nc.scalar.copy(out=result[:, e * CHUNK : (e + 1) * CHUNK], in_=banks[e][:])
+            nc.sync.dma_start(
+                out=dx_hbm[b, c * P : (c + 1) * P, 2 * half * CHUNK : 2 * (half + 1) * CHUNK], in_=result[:]
+            )
+
+        def dwd_pair(m):
+            k, second = divmod(m, 2)
+            b, j = divmod(k, PACK)
+            if second == 0:
+                dwd_bank[k] = psum.tile([P, IN_F], F32, name="dwd_bank", tag="dwd_bank", bufs=2)
+            for g in (2 * second, 2 * second + 1):
+                s = b * CHUNKS_PER_B + g
+                mx_pass(dwd_bank[k][:], by_p["g"][s], j, by_p["x"][s], g == 0, g == CHUNKS_PER_B - 1)
+
+        def u_of(k):
+            b, j = divmod(k, PACK)
+            return acc[j][:] if b == 0 else u_tile[k][:]
+
+        def scale_dwd(k):
+            b, j = divmod(k, PACK)
+            if b > 0:
+                u_tile[k] = work.tile([P, IN_F], F32, name="u", tag="u", bufs=3)
+            nc.vector.scalar_tensor_tensor(
+                out=u_of(k), in0=dwd_bank[k][:], scalar=dc_scaled[:, b, j : j + 1],
+                in1=y_wide[:, b, :], op0=MULT, op1=MULT,
+            )
+
+        def row_sum(k):
+            b, j = divmod(k, PACK)
+            products = work.tile([P, IN_F], F32, name="products", tag="products", bufs=1)
+            nc.vector.scalar_tensor_tensor(
+                out=products[:], in0=u_of(k), scalar=dc_sq_neg[:, b, j : j + 1],
+                in1=w_sb[:, j, :], op0=MULT, op1=MULT, accum_out=a_f32[:, j, b : b + 1],
+            )
+
+        def accumulate(k):
+            b, j = divmod(k, PACK)
+            if b > 0:
+                nc.vector.tensor_tensor(out=acc[j][:], in0=acc[j][:], in1=u_tile[k][:], op=ADD)
+
+        def split_high(j):
+            nc.vector.tensor_copy(out=a_split[:, j, 0:B], in_=a_f32[:, j, :])
+
+        def split_low(j):
+            nc.vector.tensor_tensor(out=a_split[:, j, B : 2 * B], in0=a_f32[:, j, :], in1=a_split[:, j, 0:B], op=SUB)
+
+        def turn_a(j):
+            bank = psum.tile([P, P], BF16, name="turn_bank", tag="turn_bank", bufs=4)
+            nc.tensor.transpose(bank[:], a_split[:, j, :], ident_bf16[:])
+            a_rows[j] = work.tile([P, P], BF16, name="a_rows", tag="a_rows", bufs=2)
+            nc.scalar.copy(out=a_rows[j][:], in_=bank[:])
+
+        def outer_sum(j):
+            r_bank[j] = psum.tile([P, IN_F], F32, name="turn_bank", tag="turn_bank", bufs=4)
+            nc.tensor.matmul(r_bank[j][:], lhsT=a_rows[j][:], rhs=y_sq_high[:], start=True, stop=False)
+            nc.tensor.matmul(r_bank[j][:], lhsT=a_rows[j][:], rhs=y_sq_low[:], start=False, stop=True)
+
+        def correction(j):
+            corr[j] = work.tile([P, IN_F], F32, name="u", tag="u", bufs=3)
+            nc.vector.tensor_tensor(out=corr[j][:], in0=r_bank[j][:], in1=w_sb[:, j, :], op=MULT)
+
+        def finish(j):
+            nc.vector.tensor_tensor(out=acc[j][:], in0=acc[j][:], in1=corr[j][:], op=ADD)
+            nc.sync.dma_start(out=dweight_hbm[:, j, :], in_=acc[j][:])
+
+        ident_f32 = keep.tile([P, P], F32)
+        ident_bf16 = keep.tile([P, P], BF16)
+        y_rows = keep.tile([P, IN_F], BF16)
+        y_sq = keep.tile([P, IN_F], F32)
+        y_sq_high = keep.tile([P, IN_F], BF16)
+        y_sq_low = keep.tile([P, IN_F], BF16)
+        y_wide = keep.tile([P, B, IN_F], BF16)
+        dc_raw = keep.tile([P, B, 2 * PACK], F32)
+        dc_scaled = keep.tile([P, B, PACK], F32)
+        dc_sq_neg = keep.tile([P, B, PACK], F32)
+        w_sb = keep.tile([P, PACK, IN_F], BF16)
+        a_f32 = keep.tile([P, PACK, B], F32)
+        a_split = keep.tile([P, PACK, P], BF16)
+        acc = [keep.tile([P, IN_F], F32, name="acc%d" % j) for j in range(PACK)]
+
+        nc.vector.memset(y_rows[:], 0.0)
+        make_identity(nc, ident_bf16[:])
+        make_identity(nc, ident_f32[:])
+        nc.gpsimd.memset(a_split[:], 0.0)
+
+        load_unit("g", 0)
+        for copy_row in (0, B):
+            nc.sync.dma_start(out=y_rows[copy_row : copy_row + B, :], in_=y[:, :])
+        nc.sync.dma_start(out=dc_raw[:, :, 0:PACK], in_=dconf.rearrange("b (q j) -> q b j", j=PACK))
+        nc.sync.dma_start(out=w_sb[:], in_=w_hbm)
+        load_unit("x", 0)
+        for n in range(1, RAW_BUFS):
+            load_unit("g", n)
+            load_unit("x", n)
+
+        nc.scalar.activation(out=y_sq[:], in_=y_rows[:], func=mybir.ActivationFunctionType.Square)
+        nc.scalar.copy(out=y_sq_high[:], in_=y_sq[:])
+        for b in range(B):
+            bank = psum.tile([P, IN_F], F32, name="dx_bank", tag="dx_bank", bufs=2)
+            nc.tensor.matmul(
+                bank[:], lhsT=ident_bf16[:, b : b + 1].to_broadcast([P, P]), rhs=y_rows[:], start=True, stop=True
+            )
+            nc.scalar.copy(out=y_wide[:, b, :], in_=bank[:])
+
+        interleave_g(0)
+        nc.vector.tensor_scalar(out=dc_scaled[:], in0=dc_raw[:, :, 0:PACK], scalar1=SCALE, scalar2=None, op0=MULT)
+        quantise_g_by_o(0)
+        nc.vector.scalar_tensor_tensor(
+            out=dc_sq_neg[:], in0=dc_scaled[:], scalar=-1.0, in1=dc_scaled[:], op0=MULT, op1=MULT
+        )
+        for j in range(PACK):
+            wd_piece(0, j)
+        nc.vector.tensor_tensor(out=y_sq_low[:], in0=y_sq[:], in1=y_sq_high[:], op=SUB)
+
+        next_unit = {"g": RAW_BUFS, "x": RAW_BUFS}
+        for s in range(N_CHUNKS):
+            b, g = divmod(s, CHUNKS_PER_B)
+            for side, kind in enumerate(("g", "x")):
+                h = 2 * s + side
+                transpose_chunk(kind, s)
+                if g < 2:
+                    wd_interleave(b, 2 * g + side)
+                if h >= DW_LAG:
+                    dwd_pair(h - DW_LAG)
+                if h >= DX_LAG:
+                    dx_pair(h - DX_LAG)
+            k = s - EPI_LAG
+            if s + 1 < N_CHUNKS:
+                interleave_g(s + 1)
+            quantise_by_p("g", s)
+            if k >= 0:
+                scale_dwd(k)
+            if s + 1 < N_CHUNKS:
+                quantise_g_by_o(s + 1)
+            if k >= 0:
+                row_sum(k)
+            quantise_by_p("x", s)
+            if k >= 0:
+                accumulate(k)
+            if b + 1 < B:
+                wd_piece(b + 1, g)
+            if g == 1:
+                wd_q[b] = quantise(wd_staged[b], E4, "wd", 2)
+            for kind in ("g", "x"):
+                n = next_unit[kind]
+                if n < len(units) and sum(units[n - RAW_BUFS]) - 1 <= s:
+                    load_unit(kind, n)
+                    next_unit[kind] = n + 1
+
+        dw_left = list(range(N_HALVES - DW_LAG, N_HALVES))
+        dx_left = list(range(N_HALVES - DX_LAG, N_HALVES))
+        first_k = N_CHUNKS - EPI_LAG
+        last_b = N_CHUNKS - PACK
+        for n in range(EPI_LAG + PACK - 1):
+            k = first_k + n
+            j = k - last_b
+            for m in dw_left[2 * n : 2 * n + 2]:
+                dwd_pair(m)
+            for m in dx_left[n : n + 1]:
+                dx_pair(m)
+            if 0 <= j - 3 < PACK:
+                outer_sum(j - 3)
+            if 0 <= j - 2 < PACK:
+                turn_a(j - 2)
+            if k < N_CHUNKS:
+                scale_dwd(k)
+            elif j - 4 < PACK:
+                correction(j - 4)
+            if 0 <= j - 1 < PACK:
+                split_high(j - 1)
+            if first_k <= k - 1 < N_CHUNKS:
+                accumulate(k - 1)
+            elif 0 <= j - 5:
+                finish(j - 5)
+            if 0 <= j - 1 < PACK:
+                split_low(j - 1)
+            if k < N_CHUNKS:
+                row_sum(k)
+        finish(PACK - 2)
+        correction(PACK - 1)
+        finish(PACK - 1)

@@ -21,11 +21,18 @@ SUB = mybir.AluOpType.subtract
 P = 128
 PACK = 4
 CHUNK = 512
+STAGE = PACK * CHUNK
 CHUNKS_PER_B = L // CHUNK
 N_CHUNKS = B * CHUNKS_PER_B
 N_HALVES = 2 * N_CHUNKS
 RAW_BUFS = 4
-DX_LAG = 7
+DX_START = 6
+DX_FULL = 12
+TB = 4
+PB = 2
+ORD = 0
+WARM = 2
+WARM_UNTIL = 9
 DW_LAG = 9
 EPI_LAG = 5
 
@@ -67,10 +74,11 @@ def tile_modulatedlinear2_v_kernel(tc, Efou, y, weight, dconf, grad_out, out_0, 
             return n, (s - units[n][0]) * CHUNK
 
         def quantise(src, fmt, tag, bufs):
-            codes = work.tile([P, CHUNK], U32, name=tag + "_codes", tag=tag + "_codes", bufs=bufs, align_bytes=64)
-            scales = work.tile([P, CHUNK], U8, name=tag + "_scales", tag=tag + "_scales", bufs=bufs, align_bytes=64)
-            nc.vector.quantize_mx(out=codes[:].bitcast(fmt), scales=scales[:], in_=src[:])
-            return codes, scales, fmt
+            width = src.shape[1] // PACK
+            codes = work.tile([P, width], U32, name=tag + "_codes", tag=tag + "_codes", bufs=bufs, align_bytes=64)
+            scales = work.tile([P, width], U8, name=tag + "_scales", tag=tag + "_scales", bufs=bufs, align_bytes=64)
+            nc.vector.quantize_mx(out=codes[:].bitcast(fmt), scales=scales[:], in_=src)
+            return [(codes[:, c : c + CHUNK], scales[:, c : c + CHUNK], fmt) for c in range(0, width, CHUNK)]
 
         def mx_pass(out, stationary, block, moving, start, stop):
             cols = slice(block * P, (block + 1) * P)
@@ -78,8 +86,8 @@ def tile_modulatedlinear2_v_kernel(tc, Efou, y, weight, dconf, grad_out, out_0, 
                 out=out,
                 lhsT=stationary[0][:, cols].bitcast(stationary[2]),
                 lhsT_scale=stationary[1][:, cols],
-                rhs=moving[0][:].bitcast(moving[2]),
-                rhs_scale=moving[1][:],
+                rhs=moving[0].bitcast(moving[2]),
+                rhs_scale=moving[1],
                 start=start,
                 stop=stop,
             )
@@ -90,23 +98,45 @@ def tile_modulatedlinear2_v_kernel(tc, Efou, y, weight, dconf, grad_out, out_0, 
                 src.rearrange("p t (c i) -> p c t i", i=4),
             )
 
-        def interleave_g(s):
-            n, off = raw_offset(s)
-            t = work.tile([P, PACK * CHUNK], BF16, name="g_grouped", tag="g_grouped", bufs=2, align_bytes=64)
-            dst, src = interleave_views(t[:], raw["g"][n][:, :, off : off + CHUNK])
-            nc.vector.tensor_copy(out=dst, in_=src)
-            staged["i", s] = t
+        def g_stage(s):
+            if s not in staged:
+                staged[s] = work.tile([P, 2 * STAGE], BF16, name="g_stage", tag="g_stage", bufs=3, align_bytes=64)
+            return staged[s]
 
-        def quantise_g_by_o(s):
-            g_by_o[s] = quantise(staged["i", s], E5, "g_by_o", 8)
+        def x_stage(pair):
+            if ("x", pair) not in staged:
+                staged["x", pair] = work.tile([P, 2 * STAGE], BF16, name="x_stage", tag="x_stage", bufs=2, align_bytes=64)
+            return staged["x", pair]
+
+        def interleave_g(s, copy, first, last):
+            n, off = raw_offset(s)
+            dst, src = interleave_views(
+                g_stage(s - 1)[:, PACK * first : PACK * last], raw["g"][n][:, :, off + first : off + last]
+            )
+            copy(out=dst, in_=src)
+
+        def quantise_g(s):
+            first = STAGE if s + 1 == N_CHUNKS else 0
+            last = STAGE if s < 0 else 2 * STAGE
+            parts = quantise(g_stage(s)[:, first:last], E5, "g", 8)
+            if s + 1 < N_CHUNKS:
+                g_by_o[s + 1] = parts[0]
+            if s >= 0:
+                by_p["g"][s] = parts[-1]
+
+        def quantise_x(pair):
+            by_p["x"][2 * pair], by_p["x"][2 * pair + 1] = quantise(x_stage(pair)[:], E4, "x", 4)
 
         def transpose_chunk(kind, s):
             n, off = raw_offset(s)
-            t = work.tile([P, PACK * CHUNK], BF16, name="turned_" + kind, tag="turned_" + kind, bufs=3, align_bytes=64)
-            t_words = t[:].bitcast(F32).rearrange("p (j q u) -> p j q u", j=PACK, u=2)
+            if kind == "g":
+                t = g_stage(s)[:, STAGE : 2 * STAGE]
+            else:
+                t = x_stage(s // 2)[:, (s % 2) * STAGE : (s % 2 + 1) * STAGE]
+            t_words = t.bitcast(F32).rearrange("p (j q u) -> p j q u", j=PACK, u=2)
             banks = []
             for pair in range(2):
-                bank = psum.tile([P, 2, 2, P], F32, name="turn_bank", tag="turn_bank", bufs=4)
+                bank = psum.tile([P, 2, 2, P], F32, name="turn_bank", tag="turn_bank", bufs=TB)
                 for jj in range(2):
                     words = raw[kind][n][:, 2 * pair + jj, off : off + CHUNK].bitcast(F32)
                     for u in range(2):
@@ -117,10 +147,6 @@ def tile_modulatedlinear2_v_kernel(tc, Efou, y, weight, dconf, grad_out, out_0, 
                     out=t_words[:, 2 * pair : 2 * pair + 2, :, :],
                     in_=banks[pair][:].rearrange("p j u q -> p j q u"),
                 )
-            staged[kind, s] = t
-
-        def quantise_by_p(kind, s):
-            by_p[kind][s] = quantise(staged[kind, s], E5 if kind == "g" else E4, kind + "_by_p", 8)
 
         def wd_piece(b, j):
             if j == 0:
@@ -132,7 +158,7 @@ def tile_modulatedlinear2_v_kernel(tc, Efou, y, weight, dconf, grad_out, out_0, 
 
         def wd_interleave(b, quarter):
             if quarter == 0:
-                wd_staged[b] = work.tile([P, PACK * IN_F], BF16, name="wd_grouped", tag="wd_grouped", bufs=2, align_bytes=64)
+                wd_staged[b] = work.tile([P, PACK * IN_F], BF16, name="wd_grouped", tag="wd_grouped", bufs=1, align_bytes=64)
             dst, src = interleave_views(
                 wd_staged[b][:, quarter * PACK * P : (quarter + 1) * PACK * P],
                 wd_rows[b][:, :, quarter * P : (quarter + 1) * P],
@@ -145,7 +171,7 @@ def tile_modulatedlinear2_v_kernel(tc, Efou, y, weight, dconf, grad_out, out_0, 
             first = b * CHUNKS_PER_B + 2 * half
             banks = []
             for e in range(2):
-                bank = psum.tile([P, CHUNK], F32, name="dx_bank", tag="dx_bank", bufs=2)
+                bank = psum.tile([P, CHUNK], F32, name="dx_bank", tag="dx_bank", bufs=PB)
                 mx_pass(bank[:], wd_q[b], c, g_by_o[first + e], True, True)
                 banks.append(bank)
             result = work.tile([P, 2 * CHUNK], F32, name="dx_out", tag="dx_out", bufs=4)
@@ -163,6 +189,18 @@ def tile_modulatedlinear2_v_kernel(tc, Efou, y, weight, dconf, grad_out, out_0, 
             for g in (2 * second, 2 * second + 1):
                 s = b * CHUNKS_PER_B + g
                 mx_pass(dwd_bank[k][:], by_p["g"][s], j, by_p["x"][s], g == 0, g == CHUNKS_PER_B - 1)
+
+        def warm():
+            for w in range(WARM):
+                bank = psum.tile([P, IN_F], F32, name="dwd_bank", tag="dwd_bank", bufs=2)
+                nc.tensor.matmul(bank[:], lhsT=ident_bf16[:], rhs=y_rows[:], start=True, stop=True)
+
+        def spread_y(b):
+            bank = psum.tile([P, IN_F], F32, name="dx_bank", tag="dx_bank", bufs=PB)
+            nc.tensor.matmul(
+                bank[:], lhsT=ident_bf16[:, b : b + 1].to_broadcast([P, P]), rhs=y_rows[:], start=True, stop=True
+            )
+            nc.scalar.copy(out=y_wide[:, b, :], in_=bank[:])
 
         def u_of(k):
             b, j = divmod(k, PACK)
@@ -197,13 +235,13 @@ def tile_modulatedlinear2_v_kernel(tc, Efou, y, weight, dconf, grad_out, out_0, 
             nc.vector.tensor_tensor(out=a_split[:, j, B : 2 * B], in0=a_f32[:, j, :], in1=a_split[:, j, 0:B], op=SUB)
 
         def turn_a(j):
-            bank = psum.tile([P, P], BF16, name="turn_bank", tag="turn_bank", bufs=4)
+            bank = psum.tile([P, P], BF16, name="turn_bank", tag="turn_bank", bufs=TB)
             nc.tensor.transpose(bank[:], a_split[:, j, :], ident_bf16[:])
             a_rows[j] = work.tile([P, P], BF16, name="a_rows", tag="a_rows", bufs=2)
             nc.scalar.copy(out=a_rows[j][:], in_=bank[:])
 
         def outer_sum(j):
-            r_bank[j] = psum.tile([P, IN_F], F32, name="turn_bank", tag="turn_bank", bufs=4)
+            r_bank[j] = psum.tile([P, IN_F], F32, name="turn_bank", tag="turn_bank", bufs=TB)
             nc.tensor.matmul(r_bank[j][:], lhsT=a_rows[j][:], rhs=y_sq_high[:], start=True, stop=False)
             nc.tensor.matmul(r_bank[j][:], lhsT=a_rows[j][:], rhs=y_sq_low[:], start=False, stop=True)
 
@@ -246,53 +284,57 @@ def tile_modulatedlinear2_v_kernel(tc, Efou, y, weight, dconf, grad_out, out_0, 
             load_unit("x", n)
 
         nc.scalar.activation(out=y_sq[:], in_=y_rows[:], func=mybir.ActivationFunctionType.Square)
-        nc.scalar.copy(out=y_sq_high[:], in_=y_sq[:])
-        for b in range(B):
-            bank = psum.tile([P, IN_F], F32, name="dx_bank", tag="dx_bank", bufs=2)
-            nc.tensor.matmul(
-                bank[:], lhsT=ident_bf16[:, b : b + 1].to_broadcast([P, P]), rhs=y_rows[:], start=True, stop=True
-            )
-            nc.scalar.copy(out=y_wide[:, b, :], in_=bank[:])
+        spread_y(0)
 
-        interleave_g(0)
+        interleave_g(0, nc.vector.tensor_copy, 0, CHUNK)
         nc.vector.tensor_scalar(out=dc_scaled[:], in0=dc_raw[:, :, 0:PACK], scalar1=SCALE, scalar2=None, op0=MULT)
-        quantise_g_by_o(0)
+        quantise_g(-1)
         nc.vector.scalar_tensor_tensor(
             out=dc_sq_neg[:], in0=dc_scaled[:], scalar=-1.0, in1=dc_scaled[:], op0=MULT, op1=MULT
         )
         for j in range(PACK):
             wd_piece(0, j)
-        nc.vector.tensor_tensor(out=y_sq_low[:], in0=y_sq[:], in1=y_sq_high[:], op=SUB)
 
+        dx_done = 0
         next_unit = {"g": RAW_BUFS, "x": RAW_BUFS}
         for s in range(N_CHUNKS):
             b, g = divmod(s, CHUNKS_PER_B)
             for side, kind in enumerate(("g", "x")):
                 h = 2 * s + side
                 transpose_chunk(kind, s)
+                if h + 1 < B:
+                    spread_y(h + 1)
+                if h == B - 1:
+                    nc.scalar.copy(out=y_sq_high[:], in_=y_sq[:])
                 if g < 2:
                     wd_interleave(b, 2 * g + side)
-                if h >= DW_LAG:
+                if h >= DW_LAG and ORD == 0:
                     dwd_pair(h - DW_LAG)
-                if h >= DX_LAG:
-                    dx_pair(h - DX_LAG)
+                if h < WARM_UNTIL:
+                    warm()
+                if h >= DX_FULL or (h >= DX_START and h % 2 == DX_START % 2):
+                    dx_pair(dx_done)
+                    dx_done = dx_done + 1
+                if h >= DW_LAG and ORD == 1:
+                    dwd_pair(h - DW_LAG)
             k = s - EPI_LAG
             if s + 1 < N_CHUNKS:
-                interleave_g(s + 1)
-            quantise_by_p("g", s)
+                interleave_g(s + 1, nc.vector.tensor_copy, 0, CHUNK)
             if k >= 0:
                 scale_dwd(k)
-            if s + 1 < N_CHUNKS:
-                quantise_g_by_o(s + 1)
-            if k >= 0:
-                row_sum(k)
-            quantise_by_p("x", s)
-            if k >= 0:
-                accumulate(k)
             if b + 1 < B:
                 wd_piece(b + 1, g)
+            if s == 2:
+                nc.vector.tensor_tensor(out=y_sq_low[:], in0=y_sq[:], in1=y_sq_high[:], op=SUB)
+            quantise_g(s)
+            if k >= 0:
+                row_sum(k)
+            if s % 2 == 1:
+                quantise_x(s // 2)
+            if k >= 0:
+                accumulate(k)
             if g == 1:
-                wd_q[b] = quantise(wd_staged[b], E4, "wd", 2)
+                wd_q[b] = quantise(wd_staged[b][:], E4, "wd", 2)[0]
             for kind in ("g", "x"):
                 n = next_unit[kind]
                 if n < len(units) and sum(units[n - RAW_BUFS]) - 1 <= s:
@@ -300,7 +342,8 @@ def tile_modulatedlinear2_v_kernel(tc, Efou, y, weight, dconf, grad_out, out_0, 
                     next_unit[kind] = n + 1
 
         dw_left = list(range(N_HALVES - DW_LAG, N_HALVES))
-        dx_left = list(range(N_HALVES - DX_LAG, N_HALVES))
+        dx_left = list(range(dx_done, N_HALVES))
+        n_tail = EPI_LAG + PACK - 1
         first_k = N_CHUNKS - EPI_LAG
         last_b = N_CHUNKS - PACK
         for n in range(EPI_LAG + PACK - 1):
@@ -308,7 +351,7 @@ def tile_modulatedlinear2_v_kernel(tc, Efou, y, weight, dconf, grad_out, out_0, 
             j = k - last_b
             for m in dw_left[2 * n : 2 * n + 2]:
                 dwd_pair(m)
-            for m in dx_left[n : n + 1]:
+            for m in dx_left[-(-n * len(dx_left) // n_tail) : -(-(n + 1) * len(dx_left) // n_tail)]:
                 dx_pair(m)
             if 0 <= j - 3 < PACK:
                 outer_sum(j - 3)

@@ -25,7 +25,11 @@ STAGE = PACK * CHUNK
 CHUNKS_PER_B = L // CHUNK
 N_CHUNKS = B * CHUNKS_PER_B
 N_HALVES = 2 * N_CHUNKS
-RAW_BUFS = 4
+CHUNK_BYTES = STAGE * 2
+YUP = 1
+OB = 5
+WV = 0
+DXN = 8
 DX_START = 6
 DX_FULL = 12
 TB = 4
@@ -45,12 +49,13 @@ def tile_modulatedlinear2_v_kernel(tc, Efou, y, weight, dconf, grad_out, out_0, 
     w_hbm = weight.rearrange("z (q j) i -> (z q) j i", j=PACK)
     dweight_hbm = out_1.rearrange("z (q j) i -> (z q) j i", j=PACK)
 
-    units = [(0, 1), (1, 1)] + [(s, 2) for s in range(2, N_CHUNKS, 2)]
+    units = [(0, 1), (1, 1), (2, 2)] + [(b * CHUNKS_PER_B, CHUNKS_PER_B) for b in range(1, B)]
     unit_of_chunk = {s: n for n, (first, count) in enumerate(units) for s in range(first, first + count)}
 
     with ExitStack() as ctx:
         keep = ctx.enter_context(tc.tile_pool(name="keep", bufs=1))
         work = ctx.enter_context(tc.tile_pool(name="work", bufs=2))
+        inputs = ctx.enter_context(tc.tile_pool(name="inputs", bufs=1))
         psum = ctx.enter_context(tc.psum_pool(name="psum", bufs=2))
         ctx.enter_context(tc.manual_schedule())
 
@@ -61,13 +66,16 @@ def tile_modulatedlinear2_v_kernel(tc, Efou, y, weight, dconf, grad_out, out_0, 
         wd_rows, wd_staged, wd_q = {}, {}, {}
         dwd_bank, u_tile, a_rows, r_bank, corr = {}, {}, {}, {}, {}
 
-        def load_unit(kind, n):
+        def load_unit(kind, n, rows):
             first, count = units[n]
             b, g = divmod(first, CHUNKS_PER_B)
             hbm = g_hbm if kind == "g" else x_hbm
-            t = work.tile([P, PACK, count * CHUNK], BF16, name="raw_" + kind, tag="raw_" + kind, bufs=RAW_BUFS)
-            nc.sync.dma_start(out=t[:], in_=hbm[b, :, :, g * CHUNK : (g + count) * CHUNK])
-            raw[kind][n] = t
+            if n not in raw[kind]:
+                slot = (2 * (kind == "x") + b % 2) * CHUNKS_PER_B + g
+                raw[kind][n] = inputs.tile(
+                    [P, PACK, count * CHUNK], BF16, name="raw_%s%d" % (kind, n), offset=slot * CHUNK_BYTES
+                )
+            nc.sync.dma_start(out=raw[kind][n][:, rows, :], in_=hbm[b, :, rows, g * CHUNK : (g + count) * CHUNK])
 
         def raw_offset(s):
             n = unit_of_chunk[s]
@@ -156,14 +164,14 @@ def tile_modulatedlinear2_v_kernel(tc, Efou, y, weight, dconf, grad_out, out_0, 
                 in1=y_wide[:, b, :], op0=MULT, op1=MULT,
             )
 
-        def wd_interleave(b, quarter):
+        def wd_interleave(b, quarter, copy):
             if quarter == 0:
                 wd_staged[b] = work.tile([P, PACK * IN_F], BF16, name="wd_grouped", tag="wd_grouped", bufs=1, align_bytes=64)
             dst, src = interleave_views(
                 wd_staged[b][:, quarter * PACK * P : (quarter + 1) * PACK * P],
                 wd_rows[b][:, :, quarter * P : (quarter + 1) * P],
             )
-            nc.scalar.copy(out=dst, in_=src)
+            copy(out=dst, in_=src)
 
         def dx_pair(m):
             b, rest = divmod(m, 8)
@@ -174,7 +182,7 @@ def tile_modulatedlinear2_v_kernel(tc, Efou, y, weight, dconf, grad_out, out_0, 
                 bank = psum.tile([P, CHUNK], F32, name="dx_bank", tag="dx_bank", bufs=PB)
                 mx_pass(bank[:], wd_q[b], c, g_by_o[first + e], True, True)
                 banks.append(bank)
-            result = work.tile([P, 2 * CHUNK], F32, name="dx_out", tag="dx_out", bufs=4)
+            result = work.tile([P, 2 * CHUNK], F32, name="dx_out", tag="dx_out", bufs=OB)
             for e in range(2):
                 nc.scalar.copy(out=result[:, e * CHUNK : (e + 1) * CHUNK], in_=banks[e][:])
             nc.sync.dma_start(
@@ -268,23 +276,29 @@ def tile_modulatedlinear2_v_kernel(tc, Efou, y, weight, dconf, grad_out, out_0, 
         a_split = keep.tile([P, PACK, P], BF16)
         acc = [keep.tile([P, IN_F], F32, name="acc%d" % j) for j in range(PACK)]
 
+        all_rows = slice(0, PACK)
+        row_halves = (slice(0, 2), slice(2, PACK))
         nc.vector.memset(y_rows[:], 0.0)
         make_identity(nc, ident_bf16[:])
         make_identity(nc, ident_f32[:])
         nc.gpsimd.memset(a_split[:], 0.0)
 
-        load_unit("g", 0)
+        load_unit("g", 0, all_rows)
         for copy_row in (0, B):
             nc.sync.dma_start(out=y_rows[copy_row : copy_row + B, :], in_=y[:, :])
         nc.sync.dma_start(out=dc_raw[:, :, 0:PACK], in_=dconf.rearrange("b (q j) -> q b j", j=PACK))
         nc.sync.dma_start(out=w_sb[:], in_=w_hbm)
-        load_unit("x", 0)
-        for n in range(1, RAW_BUFS):
-            load_unit("g", n)
-            load_unit("x", n)
+        load_unit("x", 0, all_rows)
+        for n in (1, 2):
+            load_unit("g", n, all_rows)
+            load_unit("x", n, all_rows)
+        for kind in ("g", "x"):
+            for rows in row_halves:
+                load_unit(kind, 3, rows)
 
         nc.scalar.activation(out=y_sq[:], in_=y_rows[:], func=mybir.ActivationFunctionType.Square)
-        spread_y(0)
+        for b in range(YUP):
+            spread_y(b)
 
         interleave_g(0, nc.vector.tensor_copy, 0, CHUNK)
         nc.vector.tensor_scalar(out=dc_scaled[:], in0=dc_raw[:, :, 0:PACK], scalar1=SCALE, scalar2=None, op0=MULT)
@@ -296,18 +310,17 @@ def tile_modulatedlinear2_v_kernel(tc, Efou, y, weight, dconf, grad_out, out_0, 
             wd_piece(0, j)
 
         dx_done = 0
-        next_unit = {"g": RAW_BUFS, "x": RAW_BUFS}
         for s in range(N_CHUNKS):
             b, g = divmod(s, CHUNKS_PER_B)
             for side, kind in enumerate(("g", "x")):
                 h = 2 * s + side
                 transpose_chunk(kind, s)
-                if h + 1 < B:
-                    spread_y(h + 1)
+                if h + YUP < B:
+                    spread_y(h + YUP)
                 if h == B - 1:
                     nc.scalar.copy(out=y_sq_high[:], in_=y_sq[:])
-                if g < 2:
-                    wd_interleave(b, 2 * g + side)
+                if 2 * g + side < PACK - WV:
+                    wd_interleave(b, 2 * g + side, nc.scalar.copy)
                 if h >= DW_LAG and ORD == 0:
                     dwd_pair(h - DW_LAG)
                 if h < WARM_UNTIL:
@@ -326,6 +339,9 @@ def tile_modulatedlinear2_v_kernel(tc, Efou, y, weight, dconf, grad_out, out_0, 
                 wd_piece(b + 1, g)
             if s == 2:
                 nc.vector.tensor_tensor(out=y_sq_low[:], in0=y_sq[:], in1=y_sq_high[:], op=SUB)
+            if g == 1:
+                for quarter in range(PACK - WV, PACK):
+                    wd_interleave(b, quarter, nc.vector.tensor_copy)
             quantise_g(s)
             if k >= 0:
                 row_sum(k)
@@ -335,15 +351,13 @@ def tile_modulatedlinear2_v_kernel(tc, Efou, y, weight, dconf, grad_out, out_0, 
                 accumulate(k)
             if g == 1:
                 wd_q[b] = quantise(wd_staged[b][:], E4, "wd", 2)[0]
-            for kind in ("g", "x"):
-                n = next_unit[kind]
-                if n < len(units) and sum(units[n - RAW_BUFS]) - 1 <= s:
-                    load_unit(kind, n)
-                    next_unit[kind] = n + 1
+            ahead, piece = divmod(s + 1, CHUNKS_PER_B)
+            if 1 <= ahead < B - 1:
+                load_unit("g" if piece < 2 else "x", ahead + 3, row_halves[piece % 2])
 
         dw_left = list(range(N_HALVES - DW_LAG, N_HALVES))
         dx_left = list(range(dx_done, N_HALVES))
-        n_tail = EPI_LAG + PACK - 1
+        n_tail = DXN
         first_k = N_CHUNKS - EPI_LAG
         last_b = N_CHUNKS - PACK
         for n in range(EPI_LAG + PACK - 1):

@@ -26,16 +26,16 @@ CHUNKS_PER_B = L // CHUNK
 N_CHUNKS = B * CHUNKS_PER_B
 N_HALVES = 2 * N_CHUNKS
 CHUNK_BYTES = STAGE * 2
-YUP = 1
+YUP = 2
 OB = 5
-WV = 0
+WV = 1
 DXN = 8
 DX_START = 6
-DX_FULL = 12
+DX_FULL = 10
 TB = 4
 PB = 2
 ORD = 0
-WARM = 2
+WARM = 0
 WARM_UNTIL = 9
 DW_LAG = 9
 EPI_LAG = 5
@@ -164,12 +164,12 @@ def tile_modulatedlinear2_v_kernel(tc, Efou, y, weight, dconf, grad_out, out_0, 
                 in1=y_wide[:, b, :], op0=MULT, op1=MULT,
             )
 
-        def wd_interleave(b, quarter, copy):
+        def wd_interleave(b, quarter, copy, count):
             if quarter == 0:
                 wd_staged[b] = work.tile([P, PACK * IN_F], BF16, name="wd_grouped", tag="wd_grouped", bufs=1, align_bytes=64)
             dst, src = interleave_views(
-                wd_staged[b][:, quarter * PACK * P : (quarter + 1) * PACK * P],
-                wd_rows[b][:, :, quarter * P : (quarter + 1) * P],
+                wd_staged[b][:, quarter * PACK * P : (quarter + count) * PACK * P],
+                wd_rows[b][:, :, quarter * P : (quarter + count) * P],
             )
             copy(out=dst, in_=src)
 
@@ -320,7 +320,7 @@ def tile_modulatedlinear2_v_kernel(tc, Efou, y, weight, dconf, grad_out, out_0, 
                 if h == B - 1:
                     nc.scalar.copy(out=y_sq_high[:], in_=y_sq[:])
                 if 2 * g + side < PACK - WV:
-                    wd_interleave(b, 2 * g + side, nc.scalar.copy)
+                    wd_interleave(b, 2 * g + side, nc.scalar.copy, 1)
                 if h >= DW_LAG and ORD == 0:
                     dwd_pair(h - DW_LAG)
                 if h < WARM_UNTIL:
@@ -339,9 +339,8 @@ def tile_modulatedlinear2_v_kernel(tc, Efou, y, weight, dconf, grad_out, out_0, 
                 wd_piece(b + 1, g)
             if s == 2:
                 nc.vector.tensor_tensor(out=y_sq_low[:], in0=y_sq[:], in1=y_sq_high[:], op=SUB)
-            if g == 1:
-                for quarter in range(PACK - WV, PACK):
-                    wd_interleave(b, quarter, nc.vector.tensor_copy)
+            if g == 1 and WV:
+                wd_interleave(b, PACK - WV, nc.vector.tensor_copy, WV)
             quantise_g(s)
             if k >= 0:
                 row_sum(k)

import math
from contextlib import ExitStack

import concourse.mybir as mybir
from concourse.masks import make_identity

B, L, IN_F, OUT_F = 4, 2048, 512, 512
SCALE = 1.0 / math.sqrt(IN_F)
FLOPS = 2 * 2 * B * OUT_F * IN_F * L

F32 = mybir.dt.float32
BF16 = mybir.dt.bfloat16
U32 = mybir.dt.uint32
U8 = mybir.dt.uint8
E4 = mybir.dt.float8_e4m3fn_x4
E5 = mybir.dt.float8_e5m2_x4
MULT = mybir.AluOpType.mult
ADD = mybir.AluOpType.add
SUB = mybir.AluOpType.subtract

P = 128
PACK = 4
CHUNK = 512
STAGE = PACK * CHUNK
CHUNKS_PER_B = L // CHUNK
N_CHUNKS = B * CHUNKS_PER_B
N_HALVES = 2 * N_CHUNKS
CHUNK_BYTES = STAGE * 2
YUP = 2
OB = 5
WV = 1
DXN = 8
DX_START = 6
DX_FULL = 10
TB = 4
PB = 2
ORD = 0
WARM = 0
WARM_UNTIL = 9
DW_LAG = 9
EPI_LAG = 5


def tile_modulatedlinear2_v_kernel(tc, Efou, y, weight, dconf, grad_out, out_0, out_1):
    nc = tc.nc
    g_hbm = grad_out.rearrange("b (q j a) f -> b q j (a f)", j=PACK, a=CHUNKS_PER_B)
    x_hbm = Efou.rearrange("b (c r a) f -> b r c (a f)", r=P, a=CHUNKS_PER_B)
    dx_hbm = out_0.rearrange("b (i a) f -> b i (a f)", a=CHUNKS_PER_B)
    w_hbm = weight.rearrange("z (q j) i -> (z q) j i", j=PACK)
    dweight_hbm = out_1.rearrange("z (q j) i -> (z q) j i", j=PACK)

    units = [(0, 1), (1, 1), (2, 2)] + [(b * CHUNKS_PER_B, CHUNKS_PER_B) for b in range(1, B)]
    unit_of_chunk = {s: n for n, (first, count) in enumerate(units) for s in range(first, first + count)}

    with ExitStack() as ctx:
        keep = ctx.enter_context(tc.tile_pool(name="keep", bufs=1))
        work = ctx.enter_context(tc.tile_pool(name="work", bufs=2))
        inputs = ctx.enter_context(tc.tile_pool(name="inputs", bufs=1))
        psum = ctx.enter_context(tc.psum_pool(name="psum", bufs=2))
        ctx.enter_context(tc.manual_schedule())

        raw = {"g": {}, "x": {}}
        staged = {}
        g_by_o = {}
        by_p = {"g": {}, "x": {}}
        wd_rows, wd_staged, wd_q = {}, {}, {}
        dwd_bank, u_tile, a_rows, r_bank, corr = {}, {}, {}, {}, {}

        def load_unit(kind, n, rows):
            first, count = units[n]
            b, g = divmod(first, CHUNKS_PER_B)
            hbm = g_hbm if kind == "g" else x_hbm
            if n not in raw[kind]:
                slot = (2 * (kind == "x") + b % 2) * CHUNKS_PER_B + g
                raw[kind][n] = inputs.tile(
                    [P, PACK, count * CHUNK], BF16, name="raw_%s%d" % (kind, n), offset=slot * CHUNK_BYTES
                )
            nc.sync.dma_start(out=raw[kind][n][:, rows, :], in_=hbm[b, :, rows, g * CHUNK : (g + count) * CHUNK])

        def raw_offset(s):
            n = unit_of_chunk[s]
            return n, (s - units[n][0]) * CHUNK

        def quantise(src, fmt, tag, bufs):
            width = src.shape[1] // PACK
            codes = work.tile([P, width], U32, name=tag + "_codes", tag=tag + "_codes", bufs=bufs, align_bytes=64)
            scales = work.tile([P, width], U8, name=tag + "_scales", tag=tag + "_scales", bufs=bufs, align_bytes=64)
            nc.vector.quantize_mx(out=codes[:].bitcast(fmt), scales=scales[:], in_=src)
            return [(codes[:, c : c + CHUNK], scales[:, c : c + CHUNK], fmt) for c in range(0, width, CHUNK)]

        def mx_pass(out, stationary, block, moving, start, stop):
            cols = slice(block * P, (block + 1) * P)
            nc.tensor.matmul_mx(
                out=out,
                lhsT=stationary[0][:, cols].bitcast(stationary[2]),
                lhsT_scale=stationary[1][:, cols],
                rhs=moving[0].bitcast(moving[2]),
                rhs_scale=moving[1],
                start=start,
                stop=stop,
            )

        def interleave_views(dst, src):
            return (
                dst.rearrange("p (c i t) -> p c t i", i=4, t=PACK),
                src.rearrange("p t (c i) -> p c t i", i=4),
            )

        def g_stage(s):
            if s not in staged:
                staged[s] = work.tile([P, 2 * STAGE], BF16, name="g_stage", tag="g_stage", bufs=3, align_bytes=64)
            return staged[s]

        def x_stage(pair):
            if ("x", pair) not in staged:
                staged["x", pair] = work.tile([P, 2 * STAGE], BF16, name="x_stage", tag="x_stage", bufs=2, align_bytes=64)
            return staged["x", pair]

        def interleave_g(s, copy, first, last):
            n, off = raw_offset(s)
            dst, src = interleave_views(
                g_stage(s - 1)[:, PACK * first : PACK * last], raw["g"][n][:, :, off + first : off + last]
            )
            copy(out=dst, in_=src)

        def quantise_g(s):
            first = STAGE if s + 1 == N_CHUNKS else 0
            last = STAGE if s < 0 else 2 * STAGE
            parts = quantise(g_stage(s)[:, first:last], E5, "g", 8)
            if s + 1 < N_CHUNKS:
                g_by_o[s + 1] = parts[0]
            if s >= 0:
                by_p["g"][s] = parts[-1]

        def quantise_x(pair):
            by_p["x"][2 * pair], by_p["x"][2 * pair + 1] = quantise(x_stage(pair)[:], E4, "x", 4)

        def transpose_chunk(kind, s):
            n, off = raw_offset(s)
            if kind == "g":
                t = g_stage(s)[:, STAGE : 2 * STAGE]
            else:
                t = x_stage(s // 2)[:, (s % 2) * STAGE : (s % 2 + 1) * STAGE]
            t_words = t.bitcast(F32).rearrange("p (j q u) -> p j q u", j=PACK, u=2)
            banks = []
            for pair in range(2):
                bank = psum.tile([P, 2, 2, P], F32, name="turn_bank", tag="turn_bank", bufs=TB)
                for jj in range(2):
                    words = raw[kind][n][:, 2 * pair + jj, off : off + CHUNK].bitcast(F32)
                    for u in range(2):
                        nc.tensor.transpose(bank[:, jj, u, :], words[:, u : CHUNK // 2 : 2], ident_f32[:])
                banks.append(bank)
            for pair in range(2):
                nc.scalar.copy(
                    out=t_words[:, 2 * pair : 2 * pair + 2, :, :],
                    in_=banks[pair][:].rearrange("p j u q -> p j q u"),
                )

        def wd_piece(b, j):
            if j == 0:
                wd_rows[b] = work.tile([P, PACK, IN_F], BF16, name="wd_rows", tag="wd_rows", bufs=2)
            nc.vector.scalar_tensor_tensor(
                out=wd_rows[b][:, j, :], in0=w_sb[:, j, :], scalar=dc_scaled[:, b, j : j + 1],
                in1=y_wide[:, b, :], op0=MULT, op1=MULT,
            )

        def wd_interleave(b, quarter, copy, count):
            if quarter == 0:
                wd_staged[b] = work.tile([P, PACK * IN_F], BF16, name="wd_grouped", tag="wd_grouped", bufs=1, align_bytes=64)
            dst, src = interleave_views(
                wd_staged[b][:, quarter * PACK * P : (quarter + count) * PACK * P],
                wd_rows[b][:, :, quarter * P : (quarter + count) * P],
            )
            copy(out=dst, in_=src)

        def dx_pair(m):
            b, rest = divmod(m, 8)
            half, c = divmod(rest, 4)
            first = b * CHUNKS_PER_B + 2 * half
            banks = []
            for e in range(2):
                bank = psum.tile([P, CHUNK], F32, name="dx_bank", tag="dx_bank", bufs=PB)
                mx_pass(bank[:], wd_q[b], c, g_by_o[first + e], True, True)
                banks.append(bank)
            result = work.tile([P, 2 * CHUNK], F32, name="dx_out", tag="dx_out", bufs=OB)
            for e in range(2):
                nc.scalar.copy(out=result[:, e * CHUNK : (e + 1) * CHUNK], in_=banks[e][:])
            nc.sync.dma_start(
                out=dx_hbm[b, c * P : (c + 1) * P, 2 * half * CHUNK : 2 * (half + 1) * CHUNK], in_=result[:]
            )

        def dwd_pair(m):
            k, second = divmod(m, 2)
            b, j = divmod(k, PACK)
            if second == 0:
                dwd_bank[k] = psum.tile([P, IN_F], F32, name="dwd_bank", tag="dwd_bank", bufs=2)
            for g in (2 * second, 2 * second + 1):
                s = b * CHUNKS_PER_B + g
                mx_pass(dwd_bank[k][:], by_p["g"][s], j, by_p["x"][s], g == 0, g == CHUNKS_PER_B - 1)

        def warm():
            for w in range(WARM):
                bank = psum.tile([P, IN_F], F32, name="dwd_bank", tag="dwd_bank", bufs=2)
                nc.tensor.matmul(bank[:], lhsT=ident_bf16[:], rhs=y_rows[:], start=True, stop=True)

        def spread_y(b):
            bank = psum.tile([P, IN_F], F32, name="dx_bank", tag="dx_bank", bufs=PB)
            nc.tensor.matmul(
                bank[:], lhsT=ident_bf16[:, b : b + 1].to_broadcast([P, P]), rhs=y_rows[:], start=True, stop=True
            )
            nc.scalar.copy(out=y_wide[:, b, :], in_=bank[:])

        def u_of(k):
            b, j = divmod(k, PACK)
            return acc[j][:] if b == 0 else u_tile[k][:]

        def scale_dwd(k):
            b, j = divmod(k, PACK)
            if b > 0:
                u_tile[k] = work.tile([P, IN_F], F32, name="u", tag="u", bufs=3)
            nc.vector.scalar_tensor_tensor(
                out=u_of(k), in0=dwd_bank[k][:], scalar=dc_scaled[:, b, j : j + 1],
                in1=y_wide[:, b, :], op0=MULT, op1=MULT,
            )

        def row_sum(k):
            b, j = divmod(k, PACK)
            products = work.tile([P, IN_F], F32, name="products", tag="products", bufs=1)
            nc.vector.scalar_tensor_tensor(
                out=products[:], in0=u_of(k), scalar=dc_sq_neg[:, b, j : j + 1],
                in1=w_sb[:, j, :], op0=MULT, op1=MULT, accum_out=a_f32[:, j, b : b + 1],
            )

        def accumulate(k):
            b, j = divmod(k, PACK)
            if b > 0:
                nc.vector.tensor_tensor(out=acc[j][:], in0=acc[j][:], in1=u_tile[k][:], op=ADD)

        def split_high(j):
            nc.vector.tensor_copy(out=a_split[:, j, 0:B], in_=a_f32[:, j, :])

        def split_low(j):
            nc.vector.tensor_tensor(out=a_split[:, j, B : 2 * B], in0=a_f32[:, j, :], in1=a_split[:, j, 0:B], op=SUB)

        def turn_a(j):
            bank = psum.tile([P, P], BF16, name="turn_bank", tag="turn_bank", bufs=TB)
            nc.tensor.transpose(bank[:], a_split[:, j, :], ident_bf16[:])
            a_rows[j] = work.tile([P, P], BF16, name="a_rows", tag="a_rows", bufs=2)
            nc.scalar.copy(out=a_rows[j][:], in_=bank[:])

        def outer_sum(j):
            r_bank[j] = psum.tile([P, IN_F], F32, name="turn_bank", tag="turn_bank", bufs=TB)
            nc.tensor.matmul(r_bank[j][:], lhsT=a_rows[j][:], rhs=y_sq_high[:], start=True, stop=False)
            nc.tensor.matmul(r_bank[j][:], lhsT=a_rows[j][:], rhs=y_sq_low[:], start=False, stop=True)

        def correction(j):
            corr[j] = work.tile([P, IN_F], F32, name="u", tag="u", bufs=3)
            nc.vector.tensor_tensor(out=corr[j][:], in0=r_bank[j][:], in1=w_sb[:, j, :], op=MULT)

        def finish(j):
            nc.vector.tensor_tensor(out=acc[j][:], in0=acc[j][:], in1=corr[j][:], op=ADD)
            nc.sync.dma_start(out=dweight_hbm[:, j, :], in_=acc[j][:])

        ident_f32 = keep.tile([P, P], F32)
        ident_bf16 = keep.tile([P, P], BF16)
        y_rows = keep.tile([P, IN_F], BF16)
        y_sq = keep.tile([P, IN_F], F32)
        y_sq_high = keep.tile([P, IN_F], BF16)
        y_sq_low = keep.tile([P, IN_F], BF16)
        y_wide = keep.tile([P, B, IN_F], BF16)
        dc_raw = keep.tile([P, B, 2 * PACK], F32)
        dc_scaled = keep.tile([P, B, PACK], F32)
        dc_sq_neg = keep.tile([P, B, PACK], F32)
        w_sb = keep.tile([P, PACK, IN_F], BF16)
        a_f32 = keep.tile([P, PACK, B], F32)
        a_split = keep.tile([P, PACK, P], BF16)
        acc = [keep.tile([P, IN_F], F32, name="acc%d" % j) for j in range(PACK)]

        all_rows = slice(0, PACK)
        row_halves = (slice(0, 2), slice(2, PACK))
        nc.vector.memset(y_rows[:], 0.0)
        make_identity(nc, ident_bf16[:])
        make_identity(nc, ident_f32[:])
        nc.gpsimd.memset(a_split[:], 0.0)

        load_unit("g", 0, all_rows)
        for copy_row in (0, B):
            nc.sync.dma_start(out=y_rows[copy_row : copy_row + B, :], in_=y[:, :])
        nc.sync.dma_start(out=dc_raw[:, :, 0:PACK], in_=dconf.rearrange("b (q j) -> q b j", j=PACK))
        nc.sync.dma_start(out=w_sb[:], in_=w_hbm)
        load_unit("x", 0, all_rows)
        for n in (1, 2):
            load_unit("g", n, all_rows)
            load_unit("x", n, all_rows)
        for kind in ("g", "x"):
            for rows in row_halves:
                load_unit(kind, 3, rows)

        nc.scalar.activation(out=y_sq[:], in_=y_rows[:], func=mybir.ActivationFunctionType.Square)
        for b in range(YUP):
            spread_y(b)

        interleave_g(0, nc.vector.tensor_copy, 0, CHUNK)
        nc.vector.tensor_scalar(out=dc_scaled[:], in0=dc_raw[:, :, 0:PACK], scalar1=SCALE, scalar2=None, op0=MULT)
        quantise_g(-1)
        nc.vector.scalar_tensor_tensor(
            out=dc_sq_neg[:], in0=dc_scaled[:], scalar=-1.0, in1=dc_scaled[:], op0=MULT, op1=MULT
        )
        for j in range(PACK):
            wd_piece(0, j)

        dx_done = 0
        for s in range(N_CHUNKS):
            b, g = divmod(s, CHUNKS_PER_B)
            for side, kind in enumerate(("g", "x")):
                h = 2 * s + side
                transpose_chunk(kind, s)
                if h + YUP < B:
                    spread_y(h + YUP)
                if h == B - 1:
                    nc.scalar.copy(out=y_sq_high[:], in_=y_sq[:])
                if 2 * g + side < PACK - WV:
                    wd_interleave(b, 2 * g + side, nc.scalar.copy, 1)
                if h >= DW_LAG and ORD == 0:
                    dwd_pair(h - DW_LAG)
                if h < WARM_UNTIL:
                    warm()
                if h >= DX_FULL or (h >= DX_START and h % 2 == DX_START % 2):
                    dx_pair(dx_done)
                    dx_done = dx_done + 1
                if h >= DW_LAG and ORD == 1:
                    dwd_pair(h - DW_LAG)
            k = s - EPI_LAG
            if s + 1 < N_CHUNKS:
                interleave_g(s + 1, nc.vector.tensor_copy, 0, CHUNK)
            if k >= 0:
                scale_dwd(k)
            if b + 1 < B:
                wd_piece(b + 1, g)
            if s == 2:
                nc.vector.tensor_tensor(out=y_sq_low[:], in0=y_sq[:], in1=y_sq_high[:], op=SUB)
            if g == 1 and WV:
                wd_interleave(b, PACK - WV, nc.vector.tensor_copy, WV)
            quantise_g(s)
            if k >= 0:
                row_sum(k)
            if s % 2 == 1:
                quantise_x(s // 2)
            if k >= 0:
                accumulate(k)
            if g == 1:
                wd_q[b] = quantise(wd_staged[b][:], E4, "wd", 2)[0]
            ahead, piece = divmod(s + 1, CHUNKS_PER_B)
            if 1 <= ahead < B - 1:
                load_unit("g" if piece < 2 else "x", ahead + 3, row_halves[piece % 2])

        dw_left = list(range(N_HALVES - DW_LAG, N_HALVES))
        dx_left = list(range(dx_done, N_HALVES))
        n_tail = DXN
        first_k = N_CHUNKS - EPI_LAG
        last_b = N_CHUNKS - PACK
        for n in range(EPI_LAG + PACK - 1):
            k = first_k + n
            j = k - last_b
            for m in dw_left[2 * n : 2 * n + 2]:
                dwd_pair(m)
            for m in dx_left[-(-n * len(dx_left) // n_tail) : -(-(n + 1) * len(dx_left) // n_tail)]:
                dx_pair(m)
            if 0 <= j - 3 < PACK:
                outer_sum(j - 3)
            if 0 <= j - 2 < PACK:
                turn_a(j - 2)
            if k < N_CHUNKS:
                scale_dwd(k)
            elif j - 4 < PACK:
                correction(j - 4)
            if 0 <= j - 1 < PACK:
                split_high(j - 1)
            if first_k <= k - 1 < N_CHUNKS:
                accumulate(k - 1)
            elif 0 <= j - 5:
                finish(j - 5)
            if 0 <= j - 1 < PACK:
                split_low(j - 1)
            if k < N_CHUNKS:
                row_sum(k)
        finish(PACK - 2)
        correction(PACK - 1)
        finish(PACK - 1)
